import numpy as np
import ml_dtypes

BF16 = ml_dtypes.bfloat16


def bf(x):
    return np.asarray(x, np.float32).astype(BF16)


def f32(x):
    return np.asarray(x, np.float32)


def f64(x):
    return np.asarray(x).astype(np.float64)


def striped(idx):
    return np.tile(idx.reshape(-1, 16).T, (8, 1))


D, S, N, H = 128, 1024, 384, 256


def setup_inputs():
    return {
        "embed": f32(np.random.standard_normal((D, S))),
        "pos": f32(0.5 * np.random.standard_normal((D, N))),
        "w_row": bf(0.5 * np.random.standard_normal((D, H)) / np.sqrt(D)),
        "w_col": bf(0.5 * np.random.standard_normal((D, H)) / np.sqrt(D)),
        "b1": f32(0.1 * np.random.standard_normal((H, 1))),
        "offs": striped(np.random.permutation(np.tile(np.arange(S), 2))[:N]),
    }


def reference(embed, pos, w_row, w_col, b1, offs):
    idx = offs[:16].T.reshape(-1)
    x = f64(embed)[:, idx] + f64(pos)
    a = f64(w_row).T @ x
    c = f64(w_col).T @ x + f64(b1)
    return np.concatenate([x, a, c], axis=0)

@@ -1,0 +1,65 @@
+import concourse.mybir as mybir
+
+F32, BF16, U16 = mybir.dt.float32, mybir.dt.bfloat16, mybir.dt.uint16
+ADD = mybir.AluOpType.add
+IDENTITY = mybir.ActivationFunctionType.Identity
+
+P = 128
+S = 1024
+N = 384
+H = 256
+HB = H // P
+
+FLOPS = 2 * P * (2 * H) * N
+
+
+def tile_learnedconnectmodel_kernel(tc, embed, pos, w_row, w_col, b1, offs, out):
+    nc = tc.nc
+    with (
+        tc.tile_pool(name="held", bufs=1) as held,
+        tc.psum_pool(name="psum", bufs=1) as psum,
+    ):
+        offsets = held.tile([P, N // 16], U16, name="offsets")
+        nc.sync.dma_start(offsets[:], offs)
+        table = held.tile([P, S], F32, name="table")
+        nc.scalar.dma_start(table[:], embed)
+        position = held.tile([P, N], F32, name="position")
+        nc.sync.dma_start(position[:], pos)
+        weights_row = held.tile([P, H], BF16, name="weights_row")
+        nc.scalar.dma_start(weights_row[:], w_row)
+        weights_col = held.tile([P, H], BF16, name="weights_col")
+        nc.sync.dma_start(weights_col[:], w_col)
+        bias_row = held.tile([1, H], F32, name="bias_row")
+        nc.gpsimd.dma_start(bias_row[:], b1.rearrange("h o -> o h"))
+
+        one = held.tile([1, 1], F32, name="one")
+        nc.vector.memset(one[:], 1.0)
+        bias_psum = psum.tile([P, HB], F32, name="bias_psum")
+        for h in range(HB):
+            nc.tensor.matmul(
+                bias_psum[:, h : h + 1], bias_row[:, h * P : (h + 1) * P], one[:], start=True, stop=True
+            )
+        bias_col = held.tile([P, HB], F32, name="bias_col")
+        nc.vector.tensor_copy(bias_col[:], bias_psum[:])
+
+        x = held.tile([P, N], F32, name="x")
+        nc.vector.tensor_tensor(x[:], table[:].indirect(offsets[:]), position[:], ADD)
+        nc.sync.dma_start(out[0:P, :], x[:])
+
+        x_bf16 = held.tile([P, N], BF16, name="x_bf16")
+        nc.vector.tensor_copy(x_bf16[:], x[:])
+
+        for h in range(HB):
+            block = slice(h * P, (h + 1) * P)
+
+            col_psum = psum.tile([P, N], F32, name=f"col_psum{h}")
+            nc.tensor.matmul(col_psum[:], weights_col[:, block], x_bf16[:], start=True, stop=True)
+            col_out = held.tile([P, N], F32, name=f"col_out{h}")
+            nc.scalar.activation(col_out[:], col_psum[:], IDENTITY, bias=bias_col[:, h : h + 1])
+            nc.sync.dma_start(out[P + H + h * P : P + H + (h + 1) * P, :], col_out[:])
+
+            row_psum = psum.tile([P, N], F32, name=f"row_psum{h}")
+            nc.tensor.matmul(row_psum[:], weights_row[:, block], x_bf16[:], start=True, stop=True)
+            row_out = held.tile([P, N], F32, name=f"row_out{h}")
+            nc.vector.tensor_copy(row_out[:], row_psum[:])
+            nc.sync.dma_start(out[P + h * P : P + (h + 1) * P, :], row_out[:])

@@ -23,14 +23,14 @@ def tile_learnedconnectmodel_kernel(tc, embed, pos, w_row, w_col, b1, offs, out)
         nc.sync.dma_start(offsets[:], offs)
         table = held.tile([P, S], F32, name="table")
         nc.scalar.dma_start(table[:], embed)
+        bias_row = held.tile([1, H], F32, name="bias_row")
+        nc.sync.dma_start(bias_row[:], b1.rearrange("h o -> o h"))
         position = held.tile([P, N], F32, name="position")
         nc.sync.dma_start(position[:], pos)
+        weights_col = held.tile([P, H], BF16, name="weights_col")
+        nc.scalar.dma_start(weights_col[:], w_col)
         weights_row = held.tile([P, H], BF16, name="weights_row")
         nc.scalar.dma_start(weights_row[:], w_row)
-        weights_col = held.tile([P, H], BF16, name="weights_col")
-        nc.sync.dma_start(weights_col[:], w_col)
-        bias_row = held.tile([1, H], F32, name="bias_row")
-        nc.gpsimd.dma_start(bias_row[:], b1.rearrange("h o -> o h"))
 
         one = held.tile([1, 1], F32, name="one")
         nc.vector.memset(one[:], 1.0)
@@ -40,7 +40,7 @@ def tile_learnedconnectmodel_kernel(tc, embed, pos, w_row, w_col, b1, offs, out)
                 bias_psum[:, h : h + 1], bias_row[:, h * P : (h + 1) * P], one[:], start=True, stop=True
             )
         bias_col = held.tile([P, HB], F32, name="bias_col")
-        nc.vector.tensor_copy(bias_col[:], bias_psum[:])
+        nc.scalar.activation(bias_col[:], bias_psum[:], IDENTITY)
 
         x = held.tile([P, N], F32, name="x")
         nc.vector.tensor_tensor(x[:], table[:].indirect(offsets[:]), position[:], ADD)

@@ -9,15 +9,22 @@ S = 1024
 N = 384
 H = 256
 HB = H // P
+PIECES = 3
+W = N // PIECES
+KW = W // 16
 
 FLOPS = 2 * P * (2 * H) * N
 
 
 def tile_learnedconnectmodel_kernel(tc, embed, pos, w_row, w_col, b1, offs, out):
     nc = tc.nc
+    out_row = out[P : P + H, :].rearrange("(h p) n -> p h n", p=P)
+    out_col = out[P + H : P + 2 * H, :].rearrange("(h p) n -> p h n", p=P)
     with (
         tc.tile_pool(name="held", bufs=1) as held,
-        tc.psum_pool(name="psum", bufs=1) as psum,
+        tc.tile_pool(name="pieces", bufs=PIECES) as pieces,
+        tc.psum_pool(name="bias_bank", bufs=1) as bias_bank,
+        tc.psum_pool(name="banks", bufs=PIECES) as banks,
     ):
         offsets = held.tile([P, N // 16], U16, name="offsets")
         nc.sync.dma_start(offsets[:], offs)
@@ -34,7 +41,7 @@ def tile_learnedconnectmodel_kernel(tc, embed, pos, w_row, w_col, b1, offs, out)
 
         one = held.tile([1, 1], F32, name="one")
         nc.vector.memset(one[:], 1.0)
-        bias_psum = psum.tile([P, HB], F32, name="bias_psum")
+        bias_psum = bias_bank.tile([P, HB], F32, name="bias_psum")
         for h in range(HB):
             nc.tensor.matmul(
                 bias_psum[:, h : h + 1], bias_row[:, h * P : (h + 1) * P], one[:], start=True, stop=True
@@ -42,24 +49,34 @@ def tile_learnedconnectmodel_kernel(tc, embed, pos, w_row, w_col, b1, offs, out)
         bias_col = held.tile([P, HB], F32, name="bias_col")
         nc.scalar.activation(bias_col[:], bias_psum[:], IDENTITY)
 
-        x = held.tile([P, N], F32, name="x")
-        nc.vector.tensor_tensor(x[:], table[:].indirect(offsets[:]), position[:], ADD)
-        nc.sync.dma_start(out[0:P, :], x[:])
+        col_psums, row_psums = [], []
+        for j in range(PIECES):
+            tokens = slice(j * W, (j + 1) * W)
 
-        x_bf16 = held.tile([P, N], BF16, name="x_bf16")
-        nc.vector.tensor_copy(x_bf16[:], x[:])
+            x = pieces.tile([P, W], F32, name="x")
+            looked_up = table[:].indirect(offsets[:, j * KW : (j + 1) * KW])
+            nc.vector.tensor_tensor(x[:], looked_up, position[:, tokens], ADD)
+            nc.sync.dma_start(out[0:P, tokens], x[:])
 
-        for h in range(HB):
-            block = slice(h * P, (h + 1) * P)
+            x_bf16 = pieces.tile([P, W], BF16, name="x_bf16")
+            nc.vector.tensor_copy(x_bf16[:], x[:])
 
-            col_psum = psum.tile([P, N], F32, name=f"col_psum{h}")
-            nc.tensor.matmul(col_psum[:], weights_col[:, block], x_bf16[:], start=True, stop=True)
-            col_out = held.tile([P, N], F32, name=f"col_out{h}")
-            nc.scalar.activation(col_out[:], col_psum[:], IDENTITY, bias=bias_col[:, h : h + 1])
-            nc.sync.dma_start(out[P + H + h * P : P + H + (h + 1) * P, :], col_out[:])
+            col_psum = banks.tile([P, HB, W], F32, name="col_psum")
+            row_psum = banks.tile([P, HB, W], F32, name="row_psum")
+            for weights, bank in ((weights_col, col_psum), (weights_row, row_psum)):
+                for h in range(HB):
+                    nc.tensor.matmul(bank[:, h, :], weights[:, h * P : (h + 1) * P], x_bf16[:], start=True, stop=True)
+            col_psums.append(col_psum)
+            row_psums.append(row_psum)
 
-            row_psum = psum.tile([P, N], F32, name=f"row_psum{h}")
-            nc.tensor.matmul(row_psum[:], weights_row[:, block], x_bf16[:], start=True, stop=True)
-            row_out = held.tile([P, N], F32, name=f"row_out{h}")
-            nc.vector.tensor_copy(row_out[:], row_psum[:])
-            nc.sync.dma_start(out[P + h * P : P + (h + 1) * P, :], row_out[:])
+        for j in range(PIECES):
+            tokens = slice(j * W, (j + 1) * W)
+
+            col_out = pieces.tile([P, HB, W], F32, name="col_out")
+            for h in range(HB):
+                nc.scalar.activation(col_out[:, h, :], col_psums[j][:, h, :], IDENTITY, bias=bias_col[:, h : h + 1])
+            nc.sync.dma_start(out_col[:, :, tokens], col_out[:])
+
+            row_out = pieces.tile([P, HB, W], F32, name="row_out")
+            nc.vector.tensor_copy(row_out[:], row_psums[j][:])
+            nc.sync.dma_start(out_row[:, :, tokens], row_out[:])

@@ -11,6 +11,8 @@ H = 256
 HB = H // P
 PIECES = 3
 W = N // PIECES
+WARM_MATMULS = 8
+BANK = 512
 KW = W // 16
 
 FLOPS = 2 * P * (2 * H) * N
@@ -23,6 +25,7 @@ def tile_learnedconnectmodel_kernel(tc, embed, pos, w_row, w_col, b1, offs, out)
     with (
         tc.tile_pool(name="held", bufs=1) as held,
         tc.tile_pool(name="pieces", bufs=PIECES) as pieces,
+        tc.psum_pool(name="warm_bank", bufs=1) as warm_bank,
         tc.psum_pool(name="bias_bank", bufs=1) as bias_bank,
         tc.psum_pool(name="banks", bufs=PIECES) as banks,
     ):
@@ -38,6 +41,12 @@ def tile_learnedconnectmodel_kernel(tc, embed, pos, w_row, w_col, b1, offs, out)
         nc.scalar.dma_start(weights_col[:], w_col)
         weights_row = held.tile([P, H], BF16, name="weights_row")
         nc.scalar.dma_start(weights_row[:], w_row)
+
+        zeros = held.tile([P, BANK], BF16, name="zeros")
+        nc.gpsimd.memset(zeros[:], 0.0)
+        warm_psum = warm_bank.tile([P, BANK], F32, name="warm_psum")
+        for repeat in range(WARM_MATMULS):
+            nc.tensor.matmul(warm_psum[:], zeros[:, 0:P], zeros[:], start=True, stop=True)
 
         one = held.tile([1, 1], F32, name="one")
         nc.vector.memset(one[:], 1.0)
@@ -59,7 +68,7 @@ def tile_learnedconnectmodel_kernel(tc, embed, pos, w_row, w_col, b1, offs, out)
             nc.sync.dma_start(out[0:P, tokens], x[:])
 
             x_bf16 = pieces.tile([P, W], BF16, name="x_bf16")
-            nc.vector.tensor_copy(x_bf16[:], x[:])
+            nc.scalar.activation(x_bf16[:], x[:], IDENTITY)
 
             col_psum = banks.tile([P, HB, W], F32, name="col_psum")
             row_psum = banks.tile([P, HB, W], F32, name="row_psum")

@@ -11,9 +11,8 @@ H = 256
 HB = H // P
 PIECES = 3
 W = N // PIECES
-WARM_MATMULS = 8
-BANK = 512
 KW = W // 16
+assert KW % 2 == 0
 
 FLOPS = 2 * P * (2 * H) * N
 
@@ -25,38 +24,21 @@ def tile_learnedconnectmodel_kernel(tc, embed, pos, w_row, w_col, b1, offs, out)
     with (
         tc.tile_pool(name="held", bufs=1) as held,
         tc.tile_pool(name="pieces", bufs=PIECES) as pieces,
-        tc.psum_pool(name="warm_bank", bufs=1) as warm_bank,
-        tc.psum_pool(name="bias_bank", bufs=1) as bias_bank,
         tc.psum_pool(name="banks", bufs=PIECES) as banks,
     ):
         offsets = held.tile([P, N // 16], U16, name="offsets")
         nc.sync.dma_start(offsets[:], offs)
         table = held.tile([P, S], F32, name="table")
         nc.scalar.dma_start(table[:], embed)
-        bias_row = held.tile([1, H], F32, name="bias_row")
-        nc.sync.dma_start(bias_row[:], b1.rearrange("h o -> o h"))
         position = held.tile([P, N], F32, name="position")
         nc.sync.dma_start(position[:], pos)
         weights_col = held.tile([P, H], BF16, name="weights_col")
         nc.scalar.dma_start(weights_col[:], w_col)
         weights_row = held.tile([P, H], BF16, name="weights_row")
         nc.scalar.dma_start(weights_row[:], w_row)
-
-        zeros = held.tile([P, BANK], BF16, name="zeros")
-        nc.gpsimd.memset(zeros[:], 0.0)
-        warm_psum = warm_bank.tile([P, BANK], F32, name="warm_psum")
-        for repeat in range(WARM_MATMULS):
-            nc.tensor.matmul(warm_psum[:], zeros[:, 0:P], zeros[:], start=True, stop=True)
-
-        one = held.tile([1, 1], F32, name="one")
-        nc.vector.memset(one[:], 1.0)
-        bias_psum = bias_bank.tile([P, HB], F32, name="bias_psum")
-        for h in range(HB):
-            nc.tensor.matmul(
-                bias_psum[:, h : h + 1], bias_row[:, h * P : (h + 1) * P], one[:], start=True, stop=True
-            )
         bias_col = held.tile([P, HB], F32, name="bias_col")
-        nc.scalar.activation(bias_col[:], bias_psum[:], IDENTITY)
+        with nc.allow_non_contiguous_dma(reason="b1: 256 single float32, one a partition and block"):
+            nc.sync.dma_start(bias_col[:], b1.rearrange("(h p) o -> p (h o)", p=P))
 
         col_psums, row_psums = [], []
         for j in range(PIECES):

@@ -13,6 +13,8 @@ PIECES = 3
 W = N // PIECES
 KW = W // 16
 assert KW % 2 == 0
+BANK = 512
+WARM_MATMULS = 8
 
 FLOPS = 2 * P * (2 * H) * N
 
@@ -24,6 +26,7 @@ def tile_learnedconnectmodel_kernel(tc, embed, pos, w_row, w_col, b1, offs, out)
     with (
         tc.tile_pool(name="held", bufs=1) as held,
         tc.tile_pool(name="pieces", bufs=PIECES) as pieces,
+        tc.psum_pool(name="warm_bank", bufs=1) as warm_bank,
         tc.psum_pool(name="banks", bufs=PIECES) as banks,
     ):
         offsets = held.tile([P, N // 16], U16, name="offsets")
@@ -39,6 +42,12 @@ def tile_learnedconnectmodel_kernel(tc, embed, pos, w_row, w_col, b1, offs, out)
         bias_col = held.tile([P, HB], F32, name="bias_col")
         with nc.allow_non_contiguous_dma(reason="b1: 256 single float32, one a partition and block"):
             nc.sync.dma_start(bias_col[:], b1.rearrange("(h p) o -> p (h o)", p=P))
+
+        zeros = held.tile([P, BANK], BF16, name="zeros")
+        nc.vector.memset(zeros[:], 0.0)
+        warm_psum = warm_bank.tile([P, BANK], F32, name="warm_psum")
+        for repeat in range(WARM_MATMULS):
+            nc.tensor.matmul(warm_psum[:], zeros[:, 0:P], zeros[:], start=True, stop=True)
 
         col_psums, row_psums = [], []
         for j in range(PIECES):

@@ -63,20 +63,20 @@ def tile_learnedconnectmodel_kernel(tc, embed, pos, w_row, w_col, b1, offs, out)
 
             col_psum = banks.tile([P, HB, W], F32, name="col_psum")
             row_psum = banks.tile([P, HB, W], F32, name="row_psum")
-            for weights, bank in ((weights_col, col_psum), (weights_row, row_psum)):
+            for weights, bank in ((weights_row, row_psum), (weights_col, col_psum)):
                 for h in range(HB):
                     nc.tensor.matmul(bank[:, h, :], weights[:, h * P : (h + 1) * P], x_bf16[:], start=True, stop=True)
             col_psums.append(col_psum)
             row_psums.append(row_psum)
 
+        bias_spread = bias_col[:].unsqueeze(2).to_broadcast([P, HB, W])
         for j in range(PIECES):
             tokens = slice(j * W, (j + 1) * W)
 
-            col_out = pieces.tile([P, HB, W], F32, name="col_out")
-            for h in range(HB):
-                nc.scalar.activation(col_out[:, h, :], col_psums[j][:, h, :], IDENTITY, bias=bias_col[:, h : h + 1])
-            nc.sync.dma_start(out_col[:, :, tokens], col_out[:])
-
             row_out = pieces.tile([P, HB, W], F32, name="row_out")
-            nc.vector.tensor_copy(row_out[:], row_psums[j][:])
+            nc.scalar.activation(row_out[:], row_psums[j][:], IDENTITY)
             nc.sync.dma_start(out_row[:, :, tokens], row_out[:])
+
+            col_out = pieces.tile([P, HB, W], F32, name="col_out")
+            nc.vector.tensor_tensor(col_out[:], col_psums[j][:], bias_spread, ADD)
+            nc.sync.dma_start(out_col[:, :, tokens], col_out[:])

@@ -13,6 +13,7 @@ PIECES = 3
 W = N // PIECES
 KW = W // 16
 assert KW % 2 == 0
+STORE_GROUPS = ((0,), (1, 2))
 BANK = 512
 WARM_MATMULS = 8
 
@@ -70,13 +71,13 @@ def tile_learnedconnectmodel_kernel(tc, embed, pos, w_row, w_col, b1, offs, out)
             row_psums.append(row_psum)
 
         bias_spread = bias_col[:].unsqueeze(2).to_broadcast([P, HB, W])
-        for j in range(PIECES):
-            tokens = slice(j * W, (j + 1) * W)
-
-            row_out = pieces.tile([P, HB, W], F32, name="row_out")
-            nc.scalar.activation(row_out[:], row_psums[j][:], IDENTITY)
+        for group in STORE_GROUPS:
+            tokens = slice(group[0] * W, (group[-1] + 1) * W)
+            row_out = pieces.tile([P, HB, len(group) * W], F32, name="row_out")
+            col_out = pieces.tile([P, HB, len(group) * W], F32, name="col_out")
+            for k, j in enumerate(group):
+                part = slice(k * W, (k + 1) * W)
+                nc.scalar.activation(row_out[:, :, part], row_psums[j][:], IDENTITY)
+                nc.vector.tensor_tensor(col_out[:, :, part], col_psums[j][:], bias_spread, ADD)
             nc.sync.dma_start(out_row[:, :, tokens], row_out[:])
-
-            col_out = pieces.tile([P, HB, W], F32, name="col_out")
-            nc.vector.tensor_tensor(col_out[:], col_psums[j][:], bias_spread, ADD)
             nc.sync.dma_start(out_col[:, :, tokens], col_out[:])

@@ -77,7 +77,10 @@ def tile_learnedconnectmodel_kernel(tc, embed, pos, w_row, w_col, b1, offs, out)
             col_out = pieces.tile([P, HB, len(group) * W], F32, name="col_out")
             for k, j in enumerate(group):
                 part = slice(k * W, (k + 1) * W)
-                nc.scalar.activation(row_out[:, :, part], row_psums[j][:], IDENTITY)
+                if j == 0:
+                    nc.vector.tensor_copy(row_out[:, :, part], row_psums[j][:])
+                else:
+                    nc.scalar.activation(row_out[:, :, part], row_psums[j][:], IDENTITY)
                 nc.vector.tensor_tensor(col_out[:, :, part], col_psums[j][:], bias_spread, ADD)
             nc.sync.dma_start(out_row[:, :, tokens], row_out[:])
             nc.sync.dma_start(out_col[:, :, tokens], col_out[:])

@@ -30,16 +30,17 @@ def tile_learnedconnectmodel_kernel(tc, embed, pos, w_row, w_col, b1, offs, out)
         tc.psum_pool(name="warm_bank", bufs=1) as warm_bank,
         tc.psum_pool(name="banks", bufs=PIECES) as banks,
     ):
+        table = held.tile([P, S], F32, name="table")
+        nc.sync.dma_start(table[:], embed)
         offsets = held.tile([P, N // 16], U16, name="offsets")
         nc.sync.dma_start(offsets[:], offs)
-        table = held.tile([P, S], F32, name="table")
-        nc.scalar.dma_start(table[:], embed)
         position = held.tile([P, N], F32, name="position")
-        nc.sync.dma_start(position[:], pos)
-        weights_col = held.tile([P, H], BF16, name="weights_col")
-        nc.scalar.dma_start(weights_col[:], w_col)
+        nc.sync.dma_start(position[:, 0:W], pos[:, 0:W])
+        nc.sync.dma_start(position[:, W:N], pos[:, W:N])
         weights_row = held.tile([P, H], BF16, name="weights_row")
-        nc.scalar.dma_start(weights_row[:], w_row)
+        nc.sync.dma_start(weights_row[:], w_row)
+        weights_col = held.tile([P, H], BF16, name="weights_col")
+        nc.sync.dma_start(weights_col[:], w_col)
         bias_col = held.tile([P, HB], F32, name="bias_col")
         with nc.allow_non_contiguous_dma(reason="b1: 256 single float32, one a partition and block"):
             nc.sync.dma_start(bias_col[:], b1.rearrange("(h p) o -> p (h o)", p=P))

@@ -35,11 +35,12 @@ def tile_learnedconnectmodel_kernel(tc, embed, pos, w_row, w_col, b1, offs, out)
         offsets = held.tile([P, N // 16], U16, name="offsets")
         nc.sync.dma_start(offsets[:], offs)
         position = held.tile([P, N], F32, name="position")
-        nc.sync.dma_start(position[:, 0:W], pos[:, 0:W])
-        nc.sync.dma_start(position[:, W:N], pos[:, W:N])
         weights_row = held.tile([P, H], BF16, name="weights_row")
-        nc.sync.dma_start(weights_row[:], w_row)
         weights_col = held.tile([P, H], BF16, name="weights_col")
+        nc.sync.dma_start(position[:, 0:W], pos[:, 0:W])
+        nc.sync.dma_start(position[:, W : 2 * W], pos[:, W : 2 * W])
+        nc.sync.dma_start(weights_row[:], w_row)
+        nc.sync.dma_start(position[:, 2 * W : N], pos[:, 2 * W : N])
         nc.sync.dma_start(weights_col[:], w_col)
         bias_col = held.tile([P, HB], F32, name="bias_col")
         with nc.allow_non_contiguous_dma(reason="b1: 256 single float32, one a partition and block"):
@@ -51,7 +52,7 @@ def tile_learnedconnectmodel_kernel(tc, embed, pos, w_row, w_col, b1, offs, out)
         for repeat in range(WARM_MATMULS):
             nc.tensor.matmul(warm_psum[:], zeros[:, 0:P], zeros[:], start=True, stop=True)
 
-        col_psums, row_psums = [], []
+        rounded = []
         for j in range(PIECES):
             tokens = slice(j * W, (j + 1) * W)
 
@@ -62,14 +63,17 @@ def tile_learnedconnectmodel_kernel(tc, embed, pos, w_row, w_col, b1, offs, out)
 
             x_bf16 = pieces.tile([P, W], BF16, name="x_bf16")
             nc.scalar.activation(x_bf16[:], x[:], IDENTITY)
+            rounded.append(x_bf16)
 
-            col_psum = banks.tile([P, HB, W], F32, name="col_psum")
-            row_psum = banks.tile([P, HB, W], F32, name="row_psum")
-            for weights, bank in ((weights_row, row_psum), (weights_col, col_psum)):
-                for h in range(HB):
-                    nc.tensor.matmul(bank[:, h, :], weights[:, h * P : (h + 1) * P], x_bf16[:], start=True, stop=True)
-            col_psums.append(col_psum)
-            row_psums.append(row_psum)
+        row_psums = [banks.tile([P, HB, W], F32, name="row_psum") for j in range(PIECES)]
+        col_psums = [banks.tile([P, HB, W], F32, name="col_psum") for j in range(PIECES)]
+        for group in STORE_GROUPS:
+            for weights, psums in ((weights_row, row_psums), (weights_col, col_psums)):
+                for j in group:
+                    for h in range(HB):
+                        nc.tensor.matmul(
+                            psums[j][:, h, :], weights[:, h * P : (h + 1) * P], rounded[j][:], start=True, stop=True
+                        )
 
         bias_spread = bias_col[:].unsqueeze(2).to_broadcast([P, HB, W])
         for group in STORE_GROUPS:
@@ -78,10 +82,18 @@ def tile_learnedconnectmodel_kernel(tc, embed, pos, w_row, w_col, b1, offs, out)
             col_out = pieces.tile([P, HB, len(group) * W], F32, name="col_out")
             for k, j in enumerate(group):
                 part = slice(k * W, (k + 1) * W)
-                if j == 0:
-                    nc.vector.tensor_copy(row_out[:, :, part], row_psums[j][:])
-                else:
+                if j == 1:
                     nc.scalar.activation(row_out[:, :, part], row_psums[j][:], IDENTITY)
-                nc.vector.tensor_tensor(col_out[:, :, part], col_psums[j][:], bias_spread, ADD)
+                else:
+                    nc.vector.tensor_copy(row_out[:, :, part], row_psums[j][:])
             nc.sync.dma_start(out_row[:, :, tokens], row_out[:])
+            for k, j in enumerate(group):
+                part = slice(k * W, (k + 1) * W)
+                if j == 1:
+                    for h in range(HB):
+                        nc.scalar.activation(
+                            col_out[:, h, part], col_psums[j][:, h, :], IDENTITY, bias=bias_col[:, h : h + 1]
+                        )
+                else:
+                    nc.vector.tensor_tensor(col_out[:, :, part], col_psums[j][:], bias_spread, ADD)
             nc.sync.dma_start(out_col[:, :, tokens], col_out[:])

@@ -62,18 +62,11 @@ def tile_learnedconnectmodel_kernel(tc, embed, pos, w_row, w_col, b1, offs, out)
             nc.sync.dma_start(out[0:P, tokens], x[:])
 
             x_bf16 = pieces.tile([P, W], BF16, name="x_bf16")
-            nc.scalar.activation(x_bf16[:], x[:], IDENTITY)
+            if j < PIECES - 1:
+                nc.scalar.activation(x_bf16[:], x[:], IDENTITY)
+            else:
+                nc.vector.tensor_copy(x_bf16[:], x[:])
             rounded.append(x_bf16)
-
-        row_psums = [banks.tile([P, HB, W], F32, name="row_psum") for j in range(PIECES)]
-        col_psums = [banks.tile([P, HB, W], F32, name="col_psum") for j in range(PIECES)]
-        for group in STORE_GROUPS:
-            for weights, psums in ((weights_row, row_psums), (weights_col, col_psums)):
-                for j in group:
-                    for h in range(HB):
-                        nc.tensor.matmul(
-                            psums[j][:, h, :], weights[:, h * P : (h + 1) * P], rounded[j][:], start=True, stop=True
-                        )
 
         bias_spread = bias_col[:].unsqueeze(2).to_broadcast([P, HB, W])
         for group in STORE_GROUPS:
@@ -82,18 +75,14 @@ def tile_learnedconnectmodel_kernel(tc, embed, pos, w_row, w_col, b1, offs, out)
             col_out = pieces.tile([P, HB, len(group) * W], F32, name="col_out")
             for k, j in enumerate(group):
                 part = slice(k * W, (k + 1) * W)
-                if j == 1:
-                    nc.scalar.activation(row_out[:, :, part], row_psums[j][:], IDENTITY)
-                else:
-                    nc.vector.tensor_copy(row_out[:, :, part], row_psums[j][:])
-            nc.sync.dma_start(out_row[:, :, tokens], row_out[:])
-            for k, j in enumerate(group):
-                part = slice(k * W, (k + 1) * W)
-                if j == 1:
+                row_psum = banks.tile([P, HB, W], F32, name="row_psum")
+                col_psum = banks.tile([P, HB, W], F32, name="col_psum")
+                for weights, psum in ((weights_row, row_psum), (weights_col, col_psum)):
                     for h in range(HB):
-                        nc.scalar.activation(
-                            col_out[:, h, part], col_psums[j][:, h, :], IDENTITY, bias=bias_col[:, h : h + 1]
+                        nc.tensor.matmul(
+                            psum[:, h, :], weights[:, h * P : (h + 1) * P], rounded[j][:], start=True, stop=True
                         )
-                else:
-                    nc.vector.tensor_tensor(col_out[:, :, part], col_psums[j][:], bias_spread, ADD)
+                nc.scalar.activation(row_out[:, :, part], row_psum[:], IDENTITY)
+                nc.vector.tensor_tensor(col_out[:, :, part], col_psum[:], bias_spread, ADD)
+            nc.sync.dma_start(out_row[:, :, tokens], row_out[:])
             nc.sync.dma_start(out_col[:, :, tokens], col_out[:])

@@ -22,8 +22,8 @@ FLOPS = 2 * P * (2 * H) * N
 
 def tile_learnedconnectmodel_kernel(tc, embed, pos, w_row, w_col, b1, offs, out):
     nc = tc.nc
-    out_row = out[P : P + H, :].rearrange("(h p) n -> p h n", p=P)
-    out_col = out[P + H : P + 2 * H, :].rearrange("(h p) n -> p h n", p=P)
+    out_row = out[P : P + H, :].rearrange("(p h) n -> p h n", h=HB)
+    out_col = out[P + H : P + 2 * H, :].rearrange("(p h) n -> p h n", h=HB)
     with (
         tc.tile_pool(name="held", bufs=1) as held,
         tc.tile_pool(name="pieces", bufs=PIECES) as pieces,
@@ -43,8 +43,9 @@ def tile_learnedconnectmodel_kernel(tc, embed, pos, w_row, w_col, b1, offs, out)
         nc.sync.dma_start(position[:, 2 * W : N], pos[:, 2 * W : N])
         nc.sync.dma_start(weights_col[:], w_col)
         bias_col = held.tile([P, HB], F32, name="bias_col")
-        with nc.allow_non_contiguous_dma(reason="b1: 256 single float32, one a partition and block"):
-            nc.sync.dma_start(bias_col[:], b1.rearrange("(h p) o -> p (h o)", p=P))
+        nc.sync.dma_start(bias_col[:], b1.rearrange("(p h) o -> p (h o)", h=HB))
+        blocks_row = weights_row[:].rearrange("k (p h) -> k h p", h=HB)
+        blocks_col = weights_col[:].rearrange("k (p h) -> k h p", h=HB)
 
         zeros = held.tile([P, BANK], BF16, name="zeros")
         nc.vector.memset(zeros[:], 0.0)
@@ -71,18 +72,19 @@ def tile_learnedconnectmodel_kernel(tc, embed, pos, w_row, w_col, b1, offs, out)
         bias_spread = bias_col[:].unsqueeze(2).to_broadcast([P, HB, W])
         for group in STORE_GROUPS:
             tokens = slice(group[0] * W, (group[-1] + 1) * W)
+
             row_out = pieces.tile([P, HB, len(group) * W], F32, name="row_out")
+            for k, j in enumerate(group):
+                row_psum = banks.tile([P, HB, W], F32, name="row_psum")
+                for h in range(HB):
+                    nc.tensor.matmul(row_psum[:, h, :], blocks_row[:, h, :], rounded[j][:], start=True, stop=True)
+                nc.scalar.activation(row_out[:, :, k * W : (k + 1) * W], row_psum[:], IDENTITY)
+            nc.sync.dma_start(out_row[:, :, tokens], row_out[:])
+
             col_out = pieces.tile([P, HB, len(group) * W], F32, name="col_out")
             for k, j in enumerate(group):
-                part = slice(k * W, (k + 1) * W)
-                row_psum = banks.tile([P, HB, W], F32, name="row_psum")
                 col_psum = banks.tile([P, HB, W], F32, name="col_psum")
-                for weights, psum in ((weights_row, row_psum), (weights_col, col_psum)):
-                    for h in range(HB):
-                        nc.tensor.matmul(
-                            psum[:, h, :], weights[:, h * P : (h + 1) * P], rounded[j][:], start=True, stop=True
-                        )
-                nc.scalar.activation(row_out[:, :, part], row_psum[:], IDENTITY)
-                nc.vector.tensor_tensor(col_out[:, :, part], col_psum[:], bias_spread, ADD)
-            nc.sync.dma_start(out_row[:, :, tokens], row_out[:])
+                for h in range(HB):
+                    nc.tensor.matmul(col_psum[:, h, :], blocks_col[:, h, :], rounded[j][:], start=True, stop=True)
+                nc.vector.tensor_tensor(col_out[:, :, k * W : (k + 1) * W], col_psum[:], bias_spread, ADD)
             nc.sync.dma_start(out_col[:, :, tokens], col_out[:])

@@ -28,6 +28,8 @@ def tile_learnedconnectmodel_kernel(tc, embed, pos, w_row, w_col, b1, offs, out)
         tc.tile_pool(name="held", bufs=1) as held,
         tc.tile_pool(name="pieces", bufs=PIECES) as pieces,
         tc.psum_pool(name="warm_bank", bufs=1) as warm_bank,
+        tc.psum_pool(name="first_banks", bufs=HB) as first_banks,
+        tc.psum_pool(name="row_banks", bufs=PIECES - 1) as banks_of_rows,
         tc.psum_pool(name="banks", bufs=PIECES) as banks,
     ):
         table = held.tile([P, S], F32, name="table")
@@ -74,12 +76,19 @@ def tile_learnedconnectmodel_kernel(tc, embed, pos, w_row, w_col, b1, offs, out)
             tokens = slice(group[0] * W, (group[-1] + 1) * W)
 
             row_out = pieces.tile([P, HB, len(group) * W], F32, name="row_out")
-            for k, j in enumerate(group):
-                row_psum = banks.tile([P, HB, W], F32, name="row_psum")
+            if group == STORE_GROUPS[0]:
                 for h in range(HB):
-                    nc.tensor.matmul(row_psum[:, h, :], blocks_row[:, h, :], rounded[j][:], start=True, stop=True)
-                nc.scalar.activation(row_out[:, :, k * W : (k + 1) * W], row_psum[:], IDENTITY)
-            nc.sync.dma_start(out_row[:, :, tokens], row_out[:])
+                    block_psum = first_banks.tile([P, W], F32, name="block_psum")
+                    nc.tensor.matmul(block_psum[:], blocks_row[:, h, :], rounded[group[0]][:], start=True, stop=True)
+                    nc.scalar.activation(row_out[:, h, :], block_psum[:], IDENTITY)
+                    nc.sync.dma_start(out_row[:, h, tokens], row_out[:, h, :])
+            else:
+                for k, j in enumerate(group):
+                    row_psum = banks_of_rows.tile([P, HB, W], F32, name="row_psum")
+                    for h in range(HB):
+                        nc.tensor.matmul(row_psum[:, h, :], blocks_row[:, h, :], rounded[j][:], start=True, stop=True)
+                    nc.scalar.activation(row_out[:, :, k * W : (k + 1) * W], row_psum[:], IDENTITY)
+                nc.sync.dma_start(out_row[:, :, tokens], row_out[:])
 
             col_out = pieces.tile([P, HB, len(group) * W], F32, name="col_out")
             for k, j in enumerate(group):

import concourse.mybir as mybir

F32, BF16, U16 = mybir.dt.float32, mybir.dt.bfloat16, mybir.dt.uint16
ADD = mybir.AluOpType.add
IDENTITY = mybir.ActivationFunctionType.Identity

P = 128
S = 1024
N = 384
H = 256
HB = H // P
PIECES = 3
W = N // PIECES
KW = W // 16
assert KW % 2 == 0
STORE_GROUPS = ((0,), (1, 2))
BANK = 512
WARM_MATMULS = 8

FLOPS = 2 * P * (2 * H) * N


def tile_learnedconnectmodel_kernel(tc, embed, pos, w_row, w_col, b1, offs, out):
    nc = tc.nc
    out_row = out[P : P + H, :].rearrange("(p h) n -> p h n", h=HB)
    out_col = out[P + H : P + 2 * H, :].rearrange("(p h) n -> p h n", h=HB)
    with (
        tc.tile_pool(name="held", bufs=1) as held,
        tc.tile_pool(name="pieces", bufs=PIECES) as pieces,
        tc.psum_pool(name="warm_bank", bufs=1) as warm_bank,
        tc.psum_pool(name="first_banks", bufs=HB) as first_banks,
        tc.psum_pool(name="row_banks", bufs=PIECES - 1) as banks_of_rows,
        tc.psum_pool(name="banks", bufs=PIECES) as banks,
    ):
        table = held.tile([P, S], F32, name="table")
        nc.sync.dma_start(table[:], embed)
        offsets = held.tile([P, N // 16], U16, name="offsets")
        nc.sync.dma_start(offsets[:], offs)
        position = held.tile([P, N], F32, name="position")
        weights_row = held.tile([P, H], BF16, name="weights_row")
        weights_col = held.tile([P, H], BF16, name="weights_col")
        nc.sync.dma_start(position[:, 0:W], pos[:, 0:W])
        nc.sync.dma_start(position[:, W : 2 * W], pos[:, W : 2 * W])
        nc.sync.dma_start(weights_row[:], w_row)
        nc.sync.dma_start(position[:, 2 * W : N], pos[:, 2 * W : N])
        nc.sync.dma_start(weights_col[:], w_col)
        bias_col = held.tile([P, HB], F32, name="bias_col")
        nc.sync.dma_start(bias_col[:], b1.rearrange("(p h) o -> p (h o)", h=HB))
        blocks_row = weights_row[:].rearrange("k (p h) -> k h p", h=HB)
        blocks_col = weights_col[:].rearrange("k (p h) -> k h p", h=HB)

        zeros = held.tile([P, BANK], BF16, name="zeros")
        nc.vector.memset(zeros[:], 0.0)
        warm_psum = warm_bank.tile([P, BANK], F32, name="warm_psum")
        for repeat in range(WARM_MATMULS):
            nc.tensor.matmul(warm_psum[:], zeros[:, 0:P], zeros[:], start=True, stop=True)

        rounded = []
        for j in range(PIECES):
            tokens = slice(j * W, (j + 1) * W)

            x = pieces.tile([P, W], F32, name="x")
            looked_up = table[:].indirect(offsets[:, j * KW : (j + 1) * KW])
            nc.vector.tensor_tensor(x[:], looked_up, position[:, tokens], ADD)
            nc.sync.dma_start(out[0:P, tokens], x[:])

            x_bf16 = pieces.tile([P, W], BF16, name="x_bf16")
            if j < PIECES - 1:
                nc.scalar.activation(x_bf16[:], x[:], IDENTITY)
            else:
                nc.vector.tensor_copy(x_bf16[:], x[:])
            rounded.append(x_bf16)

        bias_spread = bias_col[:].unsqueeze(2).to_broadcast([P, HB, W])
        for group in STORE_GROUPS:
            tokens = slice(group[0] * W, (group[-1] + 1) * W)

            row_out = pieces.tile([P, HB, len(group) * W], F32, name="row_out")
            if group == STORE_GROUPS[0]:
                for h in range(HB):
                    block_psum = first_banks.tile([P, W], F32, name="block_psum")
                    nc.tensor.matmul(block_psum[:], blocks_row[:, h, :], rounded[group[0]][:], start=True, stop=True)
                    nc.scalar.activation(row_out[:, h, :], block_psum[:], IDENTITY)
                    nc.sync.dma_start(out_row[:, h, tokens], row_out[:, h, :])
            else:
                for k, j in enumerate(group):
                    row_psum = banks_of_rows.tile([P, HB, W], F32, name="row_psum")
                    for h in range(HB):
                        nc.tensor.matmul(row_psum[:, h, :], blocks_row[:, h, :], rounded[j][:], start=True, stop=True)
                    nc.scalar.activation(row_out[:, :, k * W : (k + 1) * W], row_psum[:], IDENTITY)
                nc.sync.dma_start(out_row[:, :, tokens], row_out[:])

            col_out = pieces.tile([P, HB, len(group) * W], F32, name="col_out")
            for k, j in enumerate(group):
                col_psum = banks.tile([P, HB, W], F32, name="col_psum")
                for h in range(HB):
                    nc.tensor.matmul(col_psum[:, h, :], blocks_col[:, h, :], rounded[j][:], start=True, stop=True)
                nc.vector.tensor_tensor(col_out[:, :, k * W : (k + 1) * W], col_psum[:], bias_spread, ADD)
            nc.sync.dma_start(out_col[:, :, tokens], col_out[:])
